import numpy as np
import ml_dtypes

BF16 = ml_dtypes.bfloat16


def bf(x):
    return np.asarray(x, np.float32).astype(BF16)


def f32(x):
    return np.asarray(x, np.float32)


def f64(x):
    return np.asarray(x).astype(np.float64)


def striped(idx):
    return np.tile(idx.reshape(-1, 16).T, (8, 1))


S, D, R, M, N = 1024, 128, 128, 256, 512
CUTOFF = 10.0
LOG2 = np.log(2.0)


def ssp(v):
    return np.log(1.0 + np.exp(v)) - LOG2


def setup_inputs():
    return {"table": bf(np.random.standard_normal((D, S))), "w": bf(np.random.standard_normal((D, M)) / np.sqrt(D)), "rbf": bf(np.random.standard_normal((R, N))), "w1": bf(np.random.standard_normal((R, M)) / np.sqrt(R)), "b1": f32(0.1 * np.random.standard_normal((M, 1))), "w2": bf(np.random.standard_normal((M, M)) / np.sqrt(M)), "b2": f32(0.1 * np.random.standard_normal((M, 1))), "dist": f32(CUTOFF * np.random.uniform(size=(1, N))), "offs": striped(np.random.permutation(np.tile(np.arange(S), 2))[:N])}


def reference(table, w, rbf, w1, b1, w2, b2, dist, offs):
    idx = offs[:16].T.reshape(-1)
    cut = 0.5 * (np.cos(f64(dist) * (np.pi / CUTOFF)) + 1.0)
    h = ssp(f64(w1).T @ f64(rbf) + f64(b1))
    filt = (f64(w2).T @ h + f64(b2)) * cut
    nf = f64(w).T @ f64(table)[:, idx]
    return nf * filt

@@ -1,0 +1,107 @@
+import math
+
+import concourse.mybir as mybir
+
+P = 128
+NODES = 1024
+EDGES = 512
+FEATS = 256
+BLOCKS = FEATS // P
+CUTOFF = 10.0
+
+FLOPS = 2 * EDGES * (P * FEATS + FEATS * FEATS + P * FEATS)
+
+BF16, F32, U16 = mybir.dt.bfloat16, mybir.dt.float32, mybir.dt.uint16
+ACT = mybir.ActivationFunctionType
+ALU = mybir.AluOpType
+
+
+def tile_edge_update_kernel(tc, table, w, rbf, w1, b1, w2, b2, dist, offs, out):
+    nc = tc.nc
+    with (
+        tc.tile_pool(name="held", bufs=1) as held,
+        tc.psum_pool(name="psum", bufs=1) as psum,
+    ):
+        rbf_sb = held.tile([P, EDGES], BF16, name="rbf_sb")
+        nc.sync.dma_start(rbf_sb[:], rbf)
+        w1_sb = held.tile([P, FEATS], BF16, name="w1_sb")
+        nc.scalar.dma_start(w1_sb[:], w1)
+        dist_sb = held.tile([P, EDGES], F32, name="dist_sb")
+        nc.gpsimd.dma_start(dist_sb[:], dist.broadcast_to([P, EDGES]))
+        b1_sb = held.tile([P, BLOCKS], F32, name="b1_sb")
+        b2_sb = held.tile([P, BLOCKS], F32, name="b2_sb")
+        with nc.allow_non_contiguous_dma(reason="a bias element for each partition"):
+            nc.scalar.dma_start(b1_sb[:], b1.rearrange("(b p) o -> p (b o)", p=P))
+            nc.gpsimd.dma_start(b2_sb[:], b2.rearrange("(b p) o -> p (b o)", p=P))
+        offsets = held.tile([P, EDGES // 16], U16, name="offsets")
+        nc.sync.dma_start(offsets[:], offs)
+        table_sb = held.tile([P, NODES], BF16, name="table_sb")
+        nc.sync.dma_start(table_sb[:], table)
+        w_sb = held.tile([P, FEATS], BF16, name="w_sb")
+        nc.scalar.dma_start(w_sb[:], w)
+        w2_sb = held.tile([P, BLOCKS, FEATS], BF16, name="w2_sb")
+        nc.gpsimd.dma_start(w2_sb[:], w2.rearrange("(b p) m -> p b m", p=P))
+
+        cosine = held.tile([P, EDGES], F32, name="cosine")
+        nc.scalar.activation(
+            cosine[:], dist_sb[:], ACT.Sin, bias=math.pi / 2, scale=-math.pi / CUTOFF
+        )
+        cut = held.tile([P, EDGES], F32, name="cut")
+        nc.gpsimd.tensor_scalar(cut[:], cosine[:], 0.5, 0.5, ALU.mult, ALU.add)
+
+        v_ps = [psum.tile([P, EDGES], F32, name=f"v_ps{f}") for f in range(BLOCKS)]
+        for f in range(BLOCKS):
+            nc.tensor.matmul(v_ps[f][:], w1_sb[:, f * P : (f + 1) * P], rbf_sb[:], start=True, stop=True)
+
+        nf_ps = [psum.tile([P, EDGES], F32, name=f"nf_ps{m}") for m in range(BLOCKS)]
+        for m in range(BLOCKS):
+            nc.tensor.matmul(
+                nf_ps[m][:],
+                w_sb[:, m * P : (m + 1) * P],
+                table_sb[:].indirect(offsets[:]),
+                start=True,
+                stop=True,
+            )
+
+        half_b1 = held.tile([P, BLOCKS], F32, name="half_b1")
+        nc.vector.tensor_scalar_mul(half_b1[:], b1_sb[:], 0.5)
+        tanh = [held.tile([P, EDGES], F32, name=f"tanh{f}") for f in range(BLOCKS)]
+        relu = [held.tile([P, EDGES], F32, name=f"relu{f}") for f in range(BLOCKS)]
+        for f in range(BLOCKS):
+            nc.scalar.activation(
+                tanh[f][:], v_ps[f][:], ACT.Tanh, bias=half_b1[:, f : f + 1], scale=0.5
+            )
+            nc.vector.tensor_scalar(
+                relu[f][:], v_ps[f][:], b1_sb[:, f : f + 1], 0.0, ALU.add, ALU.max
+            )
+        abs_tanh = [held.tile([P, EDGES], F32, name=f"abs_tanh{f}") for f in range(BLOCKS)]
+        for f in range(BLOCKS):
+            nc.vector.scalar_tensor_tensor(
+                abs_tanh[f][:], tanh[f][:], -1.0, tanh[f][:], ALU.mult, ALU.max
+            )
+        nf_cut = [held.tile([P, EDGES], F32, name=f"nf_cut{m}") for m in range(BLOCKS)]
+        for m in range(BLOCKS):
+            nc.vector.tensor_tensor(nf_cut[m][:], nf_ps[m][:], cut[:], ALU.mult)
+        log = [held.tile([P, EDGES], F32, name=f"log{f}") for f in range(BLOCKS)]
+        h = [held.tile([P, EDGES], BF16, name=f"h{f}") for f in range(BLOCKS)]
+        for f in range(BLOCKS):
+            nc.scalar.activation(log[f][:], abs_tanh[f][:], ACT.Ln, bias=1.0, scale=1.0)
+            nc.vector.tensor_tensor(h[f][:], relu[f][:], log[f][:], ALU.subtract)
+
+        filt_ps = [psum.tile([P, EDGES], F32, name=f"filt_ps{m}") for m in range(BLOCKS)]
+        for f in range(BLOCKS):
+            for m in range(BLOCKS):
+                nc.tensor.matmul(
+                    filt_ps[m][:],
+                    w2_sb[:, f, m * P : (m + 1) * P],
+                    h[f][:],
+                    start=(f == 0),
+                    stop=(f == BLOCKS - 1),
+                )
+
+        for m in range(BLOCKS):
+            out_sb = held.tile([P, EDGES], F32, name=f"out_sb{m}")
+            nc.vector.scalar_tensor_tensor(
+                out_sb[:], filt_ps[m][:], b2_sb[:, m : m + 1], nf_cut[m][:], ALU.add, ALU.mult
+            )
+            nc.sync.dma_start(out[m * P : (m + 1) * P, :], out_sb[:])

@@ -22,6 +22,10 @@ def tile_edge_update_kernel(tc, table, w, rbf, w1, b1, w2, b2, dist, offs, out):
         tc.tile_pool(name="held", bufs=1) as held,
         tc.psum_pool(name="psum", bufs=1) as psum,
     ):
+        warm = held.tile([P, 1], F32, name="warm")
+        nc.vector.memset(warm[:], 0.0)
+        nc.scalar.activation(warm[:], warm[:], ACT.Silu)
+
         rbf_sb = held.tile([P, EDGES], BF16, name="rbf_sb")
         nc.sync.dma_start(rbf_sb[:], rbf)
         w1_sb = held.tile([P, FEATS], BF16, name="w1_sb")

@@ -8,6 +8,8 @@ EDGES = 512
 FEATS = 256
 BLOCKS = FEATS // P
 CUTOFF = 10.0
+HALF = EDGES // 2
+HALVES = [slice(0, HALF), slice(HALF, EDGES)]
 
 FLOPS = 2 * EDGES * (P * FEATS + FEATS * FEATS + P * FEATS)
 
@@ -31,12 +33,11 @@ def tile_edge_update_kernel(tc, table, w, rbf, w1, b1, w2, b2, dist, offs, out):
         w1_sb = held.tile([P, FEATS], BF16, name="w1_sb")
         nc.scalar.dma_start(w1_sb[:], w1)
         dist_sb = held.tile([P, EDGES], F32, name="dist_sb")
-        nc.gpsimd.dma_start(dist_sb[:], dist.broadcast_to([P, EDGES]))
+        nc.sync.dma_start(dist_sb[:], dist.broadcast_to([P, EDGES]))
         b1_sb = held.tile([P, BLOCKS], F32, name="b1_sb")
         b2_sb = held.tile([P, BLOCKS], F32, name="b2_sb")
         with nc.allow_non_contiguous_dma(reason="a bias element for each partition"):
             nc.scalar.dma_start(b1_sb[:], b1.rearrange("(b p) o -> p (b o)", p=P))
-            nc.gpsimd.dma_start(b2_sb[:], b2.rearrange("(b p) o -> p (b o)", p=P))
         offsets = held.tile([P, EDGES // 16], U16, name="offsets")
         nc.sync.dma_start(offsets[:], offs)
         table_sb = held.tile([P, NODES], BF16, name="table_sb")
@@ -44,7 +45,9 @@ def tile_edge_update_kernel(tc, table, w, rbf, w1, b1, w2, b2, dist, offs, out):
         w_sb = held.tile([P, FEATS], BF16, name="w_sb")
         nc.scalar.dma_start(w_sb[:], w)
         w2_sb = held.tile([P, BLOCKS, FEATS], BF16, name="w2_sb")
-        nc.gpsimd.dma_start(w2_sb[:], w2.rearrange("(b p) m -> p b m", p=P))
+        nc.sync.dma_start(w2_sb[:], w2.rearrange("(b p) m -> p b m", p=P))
+        with nc.allow_non_contiguous_dma(reason="a bias element for each partition"):
+            nc.scalar.dma_start(b2_sb[:], b2.rearrange("(b p) o -> p (b o)", p=P))
 
         cosine = held.tile([P, EDGES], F32, name="cosine")
         nc.scalar.activation(
@@ -88,24 +91,40 @@ def tile_edge_update_kernel(tc, table, w, rbf, w1, b1, w2, b2, dist, offs, out):
             nc.vector.tensor_tensor(nf_cut[m][:], nf_ps[m][:], cut[:], ALU.mult)
         log = [held.tile([P, EDGES], F32, name=f"log{f}") for f in range(BLOCKS)]
         h = [held.tile([P, EDGES], BF16, name=f"h{f}") for f in range(BLOCKS)]
-        for f in range(BLOCKS):
-            nc.scalar.activation(log[f][:], abs_tanh[f][:], ACT.Ln, bias=1.0, scale=1.0)
-            nc.vector.tensor_tensor(h[f][:], relu[f][:], log[f][:], ALU.subtract)
-
-        filt_ps = [psum.tile([P, EDGES], F32, name=f"filt_ps{m}") for m in range(BLOCKS)]
-        for f in range(BLOCKS):
-            for m in range(BLOCKS):
-                nc.tensor.matmul(
-                    filt_ps[m][:],
-                    w2_sb[:, f, m * P : (m + 1) * P],
-                    h[f][:],
-                    start=(f == 0),
-                    stop=(f == BLOCKS - 1),
+        for cols in HALVES:
+            for f in range(BLOCKS):
+                nc.scalar.activation(
+                    log[f][:, cols], abs_tanh[f][:, cols], ACT.Ln, bias=1.0, scale=1.0
+                )
+                nc.vector.tensor_tensor(
+                    h[f][:, cols], relu[f][:, cols], log[f][:, cols], ALU.subtract
                 )
 
-        for m in range(BLOCKS):
-            out_sb = held.tile([P, EDGES], F32, name=f"out_sb{m}")
-            nc.vector.scalar_tensor_tensor(
-                out_sb[:], filt_ps[m][:], b2_sb[:, m : m + 1], nf_cut[m][:], ALU.add, ALU.mult
-            )
-            nc.sync.dma_start(out[m * P : (m + 1) * P, :], out_sb[:])
+        filt_ps = [
+            [psum.tile([P, HALF], F32, name=f"filt_ps{m}{c}") for c in range(len(HALVES))]
+            for m in range(BLOCKS)
+        ]
+        for c, cols in enumerate(HALVES):
+            for f in range(BLOCKS):
+                for m in range(BLOCKS):
+                    nc.tensor.matmul(
+                        filt_ps[m][c][:],
+                        w2_sb[:, f, m * P : (m + 1) * P],
+                        h[f][:, cols],
+                        start=(f == 0),
+                        stop=(f == BLOCKS - 1),
+                    )
+
+        out_sb = [held.tile([P, EDGES], F32, name=f"out_sb{m}") for m in range(BLOCKS)]
+        for c, cols in enumerate(HALVES):
+            for m in range(BLOCKS):
+                nc.vector.scalar_tensor_tensor(
+                    out_sb[m][:, cols],
+                    filt_ps[m][c][:],
+                    b2_sb[:, m : m + 1],
+                    nf_cut[m][:, cols],
+                    ALU.add,
+                    ALU.mult,
+                )
+                store_queue = nc.sync if m == 0 else nc.scalar
+                store_queue.dma_start(out[m * P : (m + 1) * P, cols], out_sb[m][:, cols])

@@ -9,6 +9,8 @@ FEATS = 256
 BLOCKS = FEATS // P
 CUTOFF = 10.0
 HALF = EDGES // 2
+PRE_WARM = 3
+MID_WARM = 3
 HALVES = [slice(0, HALF), slice(HALF, EDGES)]
 
 FLOPS = 2 * EDGES * (P * FEATS + FEATS * FEATS + P * FEATS)
@@ -27,6 +29,9 @@ def tile_edge_update_kernel(tc, table, w, rbf, w1, b1, w2, b2, dist, offs, out):
         warm = held.tile([P, 1], F32, name="warm")
         nc.vector.memset(warm[:], 0.0)
         nc.scalar.activation(warm[:], warm[:], ACT.Silu)
+
+        zeros = held.tile([P, EDGES], BF16, name="zeros")
+        nc.gpsimd.memset(zeros[:], 0.0)
 
         rbf_sb = held.tile([P, EDGES], BF16, name="rbf_sb")
         nc.sync.dma_start(rbf_sb[:], rbf)
@@ -57,6 +62,8 @@ def tile_edge_update_kernel(tc, table, w, rbf, w1, b1, w2, b2, dist, offs, out):
         nc.gpsimd.tensor_scalar(cut[:], cosine[:], 0.5, 0.5, ALU.mult, ALU.add)
 
         v_ps = [psum.tile([P, EDGES], F32, name=f"v_ps{f}") for f in range(BLOCKS)]
+        for i in range(PRE_WARM):
+            nc.tensor.matmul(v_ps[0][:], zeros[:, :P], zeros[:], start=True, stop=True)
         for f in range(BLOCKS):
             nc.tensor.matmul(v_ps[f][:], w1_sb[:, f * P : (f + 1) * P], rbf_sb[:], start=True, stop=True)
 
@@ -89,6 +96,9 @@ def tile_edge_update_kernel(tc, table, w, rbf, w1, b1, w2, b2, dist, offs, out):
         nf_cut = [held.tile([P, EDGES], F32, name=f"nf_cut{m}") for m in range(BLOCKS)]
         for m in range(BLOCKS):
             nc.vector.tensor_tensor(nf_cut[m][:], nf_ps[m][:], cut[:], ALU.mult)
+        for i in range(MID_WARM):
+            nc.tensor.matmul(v_ps[1][:], zeros[:, :P], zeros[:], start=True, stop=True)
+
         log = [held.tile([P, EDGES], F32, name=f"log{f}") for f in range(BLOCKS)]
         h = [held.tile([P, EDGES], BF16, name=f"h{f}") for f in range(BLOCKS)]
         for cols in HALVES:

@@ -9,13 +9,12 @@ FEATS = 256
 BLOCKS = FEATS // P
 CUTOFF = 10.0
 HALF = EDGES // 2
-PRE_WARM = 3
-MID_WARM = 3
+PRE_WARM = 2
 HALVES = [slice(0, HALF), slice(HALF, EDGES)]
 
 FLOPS = 2 * EDGES * (P * FEATS + FEATS * FEATS + P * FEATS)
 
-BF16, F32, U16 = mybir.dt.bfloat16, mybir.dt.float32, mybir.dt.uint16
+BF16, F32, U16, I32 = mybir.dt.bfloat16, mybir.dt.float32, mybir.dt.uint16, mybir.dt.int32
 ACT = mybir.ActivationFunctionType
 ALU = mybir.AluOpType
 
@@ -90,46 +89,45 @@ def tile_edge_update_kernel(tc, table, w, rbf, w1, b1, w2, b2, dist, offs, out):
             )
         abs_tanh = [held.tile([P, EDGES], F32, name=f"abs_tanh{f}") for f in range(BLOCKS)]
         for f in range(BLOCKS):
-            nc.vector.scalar_tensor_tensor(
-                abs_tanh[f][:], tanh[f][:], -1.0, tanh[f][:], ALU.mult, ALU.max
+            nc.vector.tensor_scalar(
+                abs_tanh[f][:].bitcast(I32), tanh[f][:].bitcast(I32), 0x7FFFFFFF, None, ALU.bitwise_and
             )
         nf_cut = [held.tile([P, EDGES], F32, name=f"nf_cut{m}") for m in range(BLOCKS)]
         for m in range(BLOCKS):
             nc.vector.tensor_tensor(nf_cut[m][:], nf_ps[m][:], cut[:], ALU.mult)
-        for i in range(MID_WARM):
-            nc.tensor.matmul(v_ps[1][:], zeros[:, :P], zeros[:], start=True, stop=True)
+        for bank in v_ps + nf_ps:
+            nc.tensor.matmul(bank[:], zeros[:, :P], zeros[:], start=True, stop=True)
 
-        log = [held.tile([P, EDGES], F32, name=f"log{f}") for f in range(BLOCKS)]
-        h = [held.tile([P, EDGES], BF16, name=f"h{f}") for f in range(BLOCKS)]
-        for cols in HALVES:
+        h = [
+            [held.tile([P, HALF], BF16, name=f"h{f}{c}") for c in range(len(HALVES))]
+            for f in range(BLOCKS)
+        ]
+        for c, cols in enumerate(HALVES):
             for f in range(BLOCKS):
-                nc.scalar.activation(
-                    log[f][:, cols], abs_tanh[f][:, cols], ACT.Ln, bias=1.0, scale=1.0
-                )
-                nc.vector.tensor_tensor(
-                    h[f][:, cols], relu[f][:, cols], log[f][:, cols], ALU.subtract
-                )
+                log = held.tile([P, HALF], F32, name=f"log{f}{c}")
+                nc.scalar.activation(log[:], abs_tanh[f][:, cols], ACT.Ln, bias=1.0, scale=1.0)
+                nc.vector.tensor_tensor(h[f][c][:], relu[f][:, cols], log[:], ALU.subtract)
 
         filt_ps = [
             [psum.tile([P, HALF], F32, name=f"filt_ps{m}{c}") for c in range(len(HALVES))]
             for m in range(BLOCKS)
         ]
-        for c, cols in enumerate(HALVES):
+        for c in range(len(HALVES)):
             for f in range(BLOCKS):
                 for m in range(BLOCKS):
                     nc.tensor.matmul(
                         filt_ps[m][c][:],
                         w2_sb[:, f, m * P : (m + 1) * P],
-                        h[f][:, cols],
+                        h[f][c][:],
                         start=(f == 0),
                         stop=(f == BLOCKS - 1),
                     )
 
-        out_sb = [held.tile([P, EDGES], F32, name=f"out_sb{m}") for m in range(BLOCKS)]
         for c, cols in enumerate(HALVES):
             for m in range(BLOCKS):
+                out_sb = held.tile([P, HALF], F32, name=f"out_sb{m}{c}")
                 nc.vector.scalar_tensor_tensor(
-                    out_sb[m][:, cols],
+                    out_sb[:],
                     filt_ps[m][c][:],
                     b2_sb[:, m : m + 1],
                     nf_cut[m][:, cols],
@@ -137,4 +135,4 @@ def tile_edge_update_kernel(tc, table, w, rbf, w1, b1, w2, b2, dist, offs, out):
                     ALU.mult,
                 )
                 store_queue = nc.sync if m == 0 else nc.scalar
-                store_queue.dma_start(out[m * P : (m + 1) * P, cols], out_sb[m][:, cols])
+                store_queue.dma_start(out[m * P : (m + 1) * P, cols], out_sb[:])

@@ -8,13 +8,14 @@ EDGES = 512
 FEATS = 256
 BLOCKS = FEATS // P
 CUTOFF = 10.0
-HALF = EDGES // 2
-PRE_WARM = 2
-HALVES = [slice(0, HALF), slice(HALF, EDGES)]
+PIECES = 4
+PIECE = EDGES // PIECES
+PRE_WARM = 3
+MID_WARM = 3
 
 FLOPS = 2 * EDGES * (P * FEATS + FEATS * FEATS + P * FEATS)
 
-BF16, F32, U16, I32 = mybir.dt.bfloat16, mybir.dt.float32, mybir.dt.uint16, mybir.dt.int32
+BF16, F32, U16 = mybir.dt.bfloat16, mybir.dt.float32, mybir.dt.uint16
 ACT = mybir.ActivationFunctionType
 ALU = mybir.AluOpType
 
@@ -89,50 +90,56 @@ def tile_edge_update_kernel(tc, table, w, rbf, w1, b1, w2, b2, dist, offs, out):
             )
         abs_tanh = [held.tile([P, EDGES], F32, name=f"abs_tanh{f}") for f in range(BLOCKS)]
         for f in range(BLOCKS):
-            nc.vector.tensor_scalar(
-                abs_tanh[f][:].bitcast(I32), tanh[f][:].bitcast(I32), 0x7FFFFFFF, None, ALU.bitwise_and
+            nc.vector.scalar_tensor_tensor(
+                abs_tanh[f][:], tanh[f][:], -1.0, tanh[f][:], ALU.mult, ALU.max
             )
         nf_cut = [held.tile([P, EDGES], F32, name=f"nf_cut{m}") for m in range(BLOCKS)]
         for m in range(BLOCKS):
             nc.vector.tensor_tensor(nf_cut[m][:], nf_ps[m][:], cut[:], ALU.mult)
-        for bank in v_ps + nf_ps:
-            nc.tensor.matmul(bank[:], zeros[:, :P], zeros[:], start=True, stop=True)
+        for i in range(MID_WARM):
+            nc.tensor.matmul(v_ps[1][:], zeros[:, :P], zeros[:], start=True, stop=True)
 
-        h = [
-            [held.tile([P, HALF], BF16, name=f"h{f}{c}") for c in range(len(HALVES))]
-            for f in range(BLOCKS)
-        ]
-        for c, cols in enumerate(HALVES):
+        piece_cols = [slice(q * PIECE, (q + 1) * PIECE) for q in range(PIECES)]
+        log = [held.tile([P, EDGES], F32, name=f"log{f}") for f in range(BLOCKS)]
+        h = [held.tile([P, EDGES], BF16, name=f"h{f}") for f in range(BLOCKS)]
+        for cols in piece_cols:
             for f in range(BLOCKS):
-                log = held.tile([P, HALF], F32, name=f"log{f}{c}")
-                nc.scalar.activation(log[:], abs_tanh[f][:, cols], ACT.Ln, bias=1.0, scale=1.0)
-                nc.vector.tensor_tensor(h[f][c][:], relu[f][:, cols], log[:], ALU.subtract)
+                nc.scalar.activation(
+                    log[f][:, cols], abs_tanh[f][:, cols], ACT.Ln, bias=1.0, scale=1.0
+                )
+                nc.vector.tensor_tensor(
+                    h[f][:, cols], relu[f][:, cols], log[f][:, cols], ALU.subtract
+                )
 
+        bank_of_piece = ["filt_a", "filt_b", "v_ps", "nf_ps"]
         filt_ps = [
-            [psum.tile([P, HALF], F32, name=f"filt_ps{m}{c}") for c in range(len(HALVES))]
+            [
+                psum.tile([P, PIECE], F32, name=f"filt_ps{m}{q}", tag=f"{bank_of_piece[q]}{m}")
+                for q in range(PIECES)
+            ]
             for m in range(BLOCKS)
         ]
-        for c in range(len(HALVES)):
+        for q, cols in enumerate(piece_cols):
             for f in range(BLOCKS):
                 for m in range(BLOCKS):
                     nc.tensor.matmul(
-                        filt_ps[m][c][:],
+                        filt_ps[m][q][:],
                         w2_sb[:, f, m * P : (m + 1) * P],
-                        h[f][c][:],
+                        h[f][:, cols],
                         start=(f == 0),
                         stop=(f == BLOCKS - 1),
                     )
 
-        for c, cols in enumerate(HALVES):
+        out_sb = [held.tile([P, EDGES], F32, name=f"out_sb{m}") for m in range(BLOCKS)]
+        for q, cols in enumerate(piece_cols):
             for m in range(BLOCKS):
-                out_sb = held.tile([P, HALF], F32, name=f"out_sb{m}{c}")
                 nc.vector.scalar_tensor_tensor(
-                    out_sb[:],
-                    filt_ps[m][c][:],
+                    out_sb[m][:, cols],
+                    filt_ps[m][q][:],
                     b2_sb[:, m : m + 1],
                     nf_cut[m][:, cols],
                     ALU.add,
                     ALU.mult,
                 )
                 store_queue = nc.sync if m == 0 else nc.scalar
-                store_queue.dma_start(out[m * P : (m + 1) * P, cols], out_sb[:])
+                store_queue.dma_start(out[m * P : (m + 1) * P, cols], out_sb[m][:, cols])

@@ -8,10 +8,10 @@ EDGES = 512
 FEATS = 256
 BLOCKS = FEATS // P
 CUTOFF = 10.0
-PIECES = 4
-PIECE = EDGES // PIECES
-PRE_WARM = 3
-MID_WARM = 3
+HALF = EDGES // 2
+HALVES = [slice(0, HALF), slice(HALF, EDGES)]
+
+FILL_MATMULS = 3
 
 FLOPS = 2 * EDGES * (P * FEATS + FEATS * FEATS + P * FEATS)
 
@@ -26,9 +26,9 @@ def tile_edge_update_kernel(tc, table, w, rbf, w1, b1, w2, b2, dist, offs, out):
         tc.tile_pool(name="held", bufs=1) as held,
         tc.psum_pool(name="psum", bufs=1) as psum,
     ):
-        warm = held.tile([P, 1], F32, name="warm")
-        nc.vector.memset(warm[:], 0.0)
-        nc.scalar.activation(warm[:], warm[:], ACT.Silu)
+        silu_col = held.tile([P, 1], F32, name="silu_col")
+        nc.vector.memset(silu_col[:], 0.0)
+        nc.scalar.activation(silu_col[:], silu_col[:], ACT.Silu)
 
         zeros = held.tile([P, EDGES], BF16, name="zeros")
         nc.gpsimd.memset(zeros[:], 0.0)
@@ -40,8 +40,7 @@ def tile_edge_update_kernel(tc, table, w, rbf, w1, b1, w2, b2, dist, offs, out):
         dist_sb = held.tile([P, EDGES], F32, name="dist_sb")
         nc.sync.dma_start(dist_sb[:], dist.broadcast_to([P, EDGES]))
         b1_sb = held.tile([P, BLOCKS], F32, name="b1_sb")
-        b2_sb = held.tile([P, BLOCKS], F32, name="b2_sb")
-        with nc.allow_non_contiguous_dma(reason="a bias element for each partition"):
+        with nc.allow_non_contiguous_dma(reason="one bias element to a partition"):
             nc.scalar.dma_start(b1_sb[:], b1.rearrange("(b p) o -> p (b o)", p=P))
         offsets = held.tile([P, EDGES // 16], U16, name="offsets")
         nc.sync.dma_start(offsets[:], offs)
@@ -51,7 +50,8 @@ def tile_edge_update_kernel(tc, table, w, rbf, w1, b1, w2, b2, dist, offs, out):
         nc.scalar.dma_start(w_sb[:], w)
         w2_sb = held.tile([P, BLOCKS, FEATS], BF16, name="w2_sb")
         nc.sync.dma_start(w2_sb[:], w2.rearrange("(b p) m -> p b m", p=P))
-        with nc.allow_non_contiguous_dma(reason="a bias element for each partition"):
+        b2_sb = held.tile([P, BLOCKS], F32, name="b2_sb")
+        with nc.allow_non_contiguous_dma(reason="one bias element to a partition"):
             nc.scalar.dma_start(b2_sb[:], b2.rearrange("(b p) o -> p (b o)", p=P))
 
         cosine = held.tile([P, EDGES], F32, name="cosine")
@@ -61,11 +61,13 @@ def tile_edge_update_kernel(tc, table, w, rbf, w1, b1, w2, b2, dist, offs, out):
         cut = held.tile([P, EDGES], F32, name="cut")
         nc.gpsimd.tensor_scalar(cut[:], cosine[:], 0.5, 0.5, ALU.mult, ALU.add)
 
-        v_ps = [psum.tile([P, EDGES], F32, name=f"v_ps{f}") for f in range(BLOCKS)]
-        for i in range(PRE_WARM):
-            nc.tensor.matmul(v_ps[0][:], zeros[:, :P], zeros[:], start=True, stop=True)
+        lin1_ps = [psum.tile([P, EDGES], F32, name=f"lin1_ps{f}") for f in range(BLOCKS)]
+        for fill in range(FILL_MATMULS):
+            nc.tensor.matmul(lin1_ps[0][:], zeros[:, :P], zeros[:], start=True, stop=True)
         for f in range(BLOCKS):
-            nc.tensor.matmul(v_ps[f][:], w1_sb[:, f * P : (f + 1) * P], rbf_sb[:], start=True, stop=True)
+            nc.tensor.matmul(
+                lin1_ps[f][:], w1_sb[:, f * P : (f + 1) * P], rbf_sb[:], start=True, stop=True
+            )
 
         nf_ps = [psum.tile([P, EDGES], F32, name=f"nf_ps{m}") for m in range(BLOCKS)]
         for m in range(BLOCKS):
@@ -83,10 +85,10 @@ def tile_edge_update_kernel(tc, table, w, rbf, w1, b1, w2, b2, dist, offs, out):
         relu = [held.tile([P, EDGES], F32, name=f"relu{f}") for f in range(BLOCKS)]
         for f in range(BLOCKS):
             nc.scalar.activation(
-                tanh[f][:], v_ps[f][:], ACT.Tanh, bias=half_b1[:, f : f + 1], scale=0.5
+                tanh[f][:], lin1_ps[f][:], ACT.Tanh, bias=half_b1[:, f : f + 1], scale=0.5
             )
             nc.vector.tensor_scalar(
-                relu[f][:], v_ps[f][:], b1_sb[:, f : f + 1], 0.0, ALU.add, ALU.max
+                relu[f][:], lin1_ps[f][:], b1_sb[:, f : f + 1], 0.0, ALU.add, ALU.max
             )
         abs_tanh = [held.tile([P, EDGES], F32, name=f"abs_tanh{f}") for f in range(BLOCKS)]
         for f in range(BLOCKS):
@@ -96,13 +98,13 @@ def tile_edge_update_kernel(tc, table, w, rbf, w1, b1, w2, b2, dist, offs, out):
         nf_cut = [held.tile([P, EDGES], F32, name=f"nf_cut{m}") for m in range(BLOCKS)]
         for m in range(BLOCKS):
             nc.vector.tensor_tensor(nf_cut[m][:], nf_ps[m][:], cut[:], ALU.mult)
-        for i in range(MID_WARM):
-            nc.tensor.matmul(v_ps[1][:], zeros[:, :P], zeros[:], start=True, stop=True)
 
-        piece_cols = [slice(q * PIECE, (q + 1) * PIECE) for q in range(PIECES)]
+        for fill in range(FILL_MATMULS):
+            nc.tensor.matmul(lin1_ps[1][:], zeros[:, :P], zeros[:], start=True, stop=True)
+
         log = [held.tile([P, EDGES], F32, name=f"log{f}") for f in range(BLOCKS)]
         h = [held.tile([P, EDGES], BF16, name=f"h{f}") for f in range(BLOCKS)]
-        for cols in piece_cols:
+        for cols in HALVES:
             for f in range(BLOCKS):
                 nc.scalar.activation(
                     log[f][:, cols], abs_tanh[f][:, cols], ACT.Ln, bias=1.0, scale=1.0
@@ -111,35 +113,31 @@ def tile_edge_update_kernel(tc, table, w, rbf, w1, b1, w2, b2, dist, offs, out):
                     h[f][:, cols], relu[f][:, cols], log[f][:, cols], ALU.subtract
                 )
 
-        bank_of_piece = ["filt_a", "filt_b", "v_ps", "nf_ps"]
-        filt_ps = [
-            [
-                psum.tile([P, PIECE], F32, name=f"filt_ps{m}{q}", tag=f"{bank_of_piece[q]}{m}")
-                for q in range(PIECES)
-            ]
+        lin2_ps = [
+            [psum.tile([P, HALF], F32, name=f"lin2_ps{m}{c}") for c in range(len(HALVES))]
             for m in range(BLOCKS)
         ]
-        for q, cols in enumerate(piece_cols):
+        for c, cols in enumerate(HALVES):
             for f in range(BLOCKS):
                 for m in range(BLOCKS):
                     nc.tensor.matmul(
-                        filt_ps[m][q][:],
+                        lin2_ps[m][c][:],
                         w2_sb[:, f, m * P : (m + 1) * P],
                         h[f][:, cols],
                         start=(f == 0),
                         stop=(f == BLOCKS - 1),
                     )
 
+        store_queues = [nc.sync, nc.scalar]
         out_sb = [held.tile([P, EDGES], F32, name=f"out_sb{m}") for m in range(BLOCKS)]
-        for q, cols in enumerate(piece_cols):
+        for c, cols in enumerate(HALVES):
             for m in range(BLOCKS):
                 nc.vector.scalar_tensor_tensor(
                     out_sb[m][:, cols],
-                    filt_ps[m][q][:],
+                    lin2_ps[m][c][:],
                     b2_sb[:, m : m + 1],
                     nf_cut[m][:, cols],
                     ALU.add,
                     ALU.mult,
                 )
-                store_queue = nc.sync if m == 0 else nc.scalar
-                store_queue.dma_start(out[m * P : (m + 1) * P, cols], out_sb[m][:, cols])
+                store_queues[m].dma_start(out[m * P : (m + 1) * P, cols], out_sb[m][:, cols])

@@ -13,9 +13,11 @@ HALVES = [slice(0, HALF), slice(HALF, EDGES)]
 
 FILL_MATMULS = 3
 
+ALL_BUT_SIGN = 0x7FFFFFFF
+
 FLOPS = 2 * EDGES * (P * FEATS + FEATS * FEATS + P * FEATS)
 
-BF16, F32, U16 = mybir.dt.bfloat16, mybir.dt.float32, mybir.dt.uint16
+BF16, F32, I32, U16 = mybir.dt.bfloat16, mybir.dt.float32, mybir.dt.int32, mybir.dt.uint16
 ACT = mybir.ActivationFunctionType
 ALU = mybir.AluOpType
 
@@ -58,8 +60,8 @@ def tile_edge_update_kernel(tc, table, w, rbf, w1, b1, w2, b2, dist, offs, out):
         nc.scalar.activation(
             cosine[:], dist_sb[:], ACT.Sin, bias=math.pi / 2, scale=-math.pi / CUTOFF
         )
-        cut = held.tile([P, EDGES], F32, name="cut")
-        nc.gpsimd.tensor_scalar(cut[:], cosine[:], 0.5, 0.5, ALU.mult, ALU.add)
+        half_w = held.tile([P, FEATS], BF16, name="half_w")
+        nc.vector.tensor_scalar_mul(half_w[:], w_sb[:], 0.5)
 
         lin1_ps = [psum.tile([P, EDGES], F32, name=f"lin1_ps{f}") for f in range(BLOCKS)]
         for fill in range(FILL_MATMULS):
@@ -69,11 +71,11 @@ def tile_edge_update_kernel(tc, table, w, rbf, w1, b1, w2, b2, dist, offs, out):
                 lin1_ps[f][:], w1_sb[:, f * P : (f + 1) * P], rbf_sb[:], start=True, stop=True
             )
 
-        nf_ps = [psum.tile([P, EDGES], F32, name=f"nf_ps{m}") for m in range(BLOCKS)]
+        half_nf_ps = [psum.tile([P, EDGES], F32, name=f"half_nf_ps{m}") for m in range(BLOCKS)]
         for m in range(BLOCKS):
             nc.tensor.matmul(
-                nf_ps[m][:],
-                w_sb[:, m * P : (m + 1) * P],
+                half_nf_ps[m][:],
+                half_w[:, m * P : (m + 1) * P],
                 table_sb[:].indirect(offsets[:]),
                 start=True,
                 stop=True,
@@ -83,21 +85,26 @@ def tile_edge_update_kernel(tc, table, w, rbf, w1, b1, w2, b2, dist, offs, out):
         nc.vector.tensor_scalar_mul(half_b1[:], b1_sb[:], 0.5)
         tanh = [held.tile([P, EDGES], F32, name=f"tanh{f}") for f in range(BLOCKS)]
         relu = [held.tile([P, EDGES], F32, name=f"relu{f}") for f in range(BLOCKS)]
+        abs_tanh = [held.tile([P, EDGES], F32, name=f"abs_tanh{f}") for f in range(BLOCKS)]
         for f in range(BLOCKS):
             nc.scalar.activation(
                 tanh[f][:], lin1_ps[f][:], ACT.Tanh, bias=half_b1[:, f : f + 1], scale=0.5
             )
             nc.vector.tensor_scalar(
-                relu[f][:], lin1_ps[f][:], b1_sb[:, f : f + 1], 0.0, ALU.add, ALU.max
+                abs_tanh[f][:].bitcast(I32),
+                tanh[f][:].bitcast(I32),
+                ALL_BUT_SIGN,
+                None,
+                ALU.bitwise_and,
             )
-        abs_tanh = [held.tile([P, EDGES], F32, name=f"abs_tanh{f}") for f in range(BLOCKS)]
-        for f in range(BLOCKS):
-            nc.vector.scalar_tensor_tensor(
-                abs_tanh[f][:], tanh[f][:], -1.0, tanh[f][:], ALU.mult, ALU.max
+            nc.vector.tensor_scalar(
+                relu[f][:], lin1_ps[f][:], b1_sb[:, f : f + 1], 0.0, ALU.add, ALU.max
             )
         nf_cut = [held.tile([P, EDGES], F32, name=f"nf_cut{m}") for m in range(BLOCKS)]
         for m in range(BLOCKS):
-            nc.vector.tensor_tensor(nf_cut[m][:], nf_ps[m][:], cut[:], ALU.mult)
+            nc.vector.scalar_tensor_tensor(
+                nf_cut[m][:], cosine[:], 1.0, half_nf_ps[m][:], ALU.add, ALU.mult
+            )
 
         for fill in range(FILL_MATMULS):
             nc.tensor.matmul(lin1_ps[1][:], zeros[:, :P], zeros[:], start=True, stop=True)

@@ -54,7 +54,7 @@ def tile_edge_update_kernel(tc, table, w, rbf, w1, b1, w2, b2, dist, offs, out):
         nc.sync.dma_start(w2_sb[:], w2.rearrange("(b p) m -> p b m", p=P))
         b2_sb = held.tile([P, BLOCKS], F32, name="b2_sb")
         with nc.allow_non_contiguous_dma(reason="one bias element to a partition"):
-            nc.scalar.dma_start(b2_sb[:], b2.rearrange("(b p) o -> p (b o)", p=P))
+            nc.sync.dma_start(b2_sb[:], b2.rearrange("(b p) o -> p (b o)", p=P))
 
         cosine = held.tile([P, EDGES], F32, name="cosine")
         nc.scalar.activation(

@@ -38,18 +38,18 @@ def tile_edge_update_kernel(tc, table, w, rbf, w1, b1, w2, b2, dist, offs, out):
         rbf_sb = held.tile([P, EDGES], BF16, name="rbf_sb")
         nc.sync.dma_start(rbf_sb[:], rbf)
         w1_sb = held.tile([P, FEATS], BF16, name="w1_sb")
-        nc.scalar.dma_start(w1_sb[:], w1)
-        dist_sb = held.tile([P, EDGES], F32, name="dist_sb")
-        nc.sync.dma_start(dist_sb[:], dist.broadcast_to([P, EDGES]))
+        nc.sync.dma_start(w1_sb[:], w1)
         b1_sb = held.tile([P, BLOCKS], F32, name="b1_sb")
         with nc.allow_non_contiguous_dma(reason="one bias element to a partition"):
-            nc.scalar.dma_start(b1_sb[:], b1.rearrange("(b p) o -> p (b o)", p=P))
+            nc.sync.dma_start(b1_sb[:], b1.rearrange("(b p) o -> p (b o)", p=P))
+        dist_sb = held.tile([P, EDGES], F32, name="dist_sb")
+        nc.sync.dma_start(dist_sb[:], dist.broadcast_to([P, EDGES]))
+        w_sb = held.tile([P, FEATS], BF16, name="w_sb")
+        nc.sync.dma_start(w_sb[:], w)
         offsets = held.tile([P, EDGES // 16], U16, name="offsets")
         nc.sync.dma_start(offsets[:], offs)
         table_sb = held.tile([P, NODES], BF16, name="table_sb")
         nc.sync.dma_start(table_sb[:], table)
-        w_sb = held.tile([P, FEATS], BF16, name="w_sb")
-        nc.scalar.dma_start(w_sb[:], w)
         w2_sb = held.tile([P, BLOCKS, FEATS], BF16, name="w2_sb")
         nc.sync.dma_start(w2_sb[:], w2.rearrange("(b p) m -> p b m", p=P))
         b2_sb = held.tile([P, BLOCKS], F32, name="b2_sb")

@@ -56,13 +56,6 @@ def tile_edge_update_kernel(tc, table, w, rbf, w1, b1, w2, b2, dist, offs, out):
         with nc.allow_non_contiguous_dma(reason="one bias element to a partition"):
             nc.sync.dma_start(b2_sb[:], b2.rearrange("(b p) o -> p (b o)", p=P))
 
-        cosine = held.tile([P, EDGES], F32, name="cosine")
-        nc.scalar.activation(
-            cosine[:], dist_sb[:], ACT.Sin, bias=math.pi / 2, scale=-math.pi / CUTOFF
-        )
-        half_w = held.tile([P, FEATS], BF16, name="half_w")
-        nc.vector.tensor_scalar_mul(half_w[:], w_sb[:], 0.5)
-
         lin1_ps = [psum.tile([P, EDGES], F32, name=f"lin1_ps{f}") for f in range(BLOCKS)]
         for fill in range(FILL_MATMULS):
             nc.tensor.matmul(lin1_ps[0][:], zeros[:, :P], zeros[:], start=True, stop=True)
@@ -71,6 +64,8 @@ def tile_edge_update_kernel(tc, table, w, rbf, w1, b1, w2, b2, dist, offs, out):
                 lin1_ps[f][:], w1_sb[:, f * P : (f + 1) * P], rbf_sb[:], start=True, stop=True
             )
 
+        half_w = held.tile([P, FEATS], BF16, name="half_w")
+        nc.vector.tensor_scalar_mul(half_w[:], w_sb[:], 0.5)
         half_nf_ps = [psum.tile([P, EDGES], F32, name=f"half_nf_ps{m}") for m in range(BLOCKS)]
         for m in range(BLOCKS):
             nc.tensor.matmul(
@@ -100,6 +95,11 @@ def tile_edge_update_kernel(tc, table, w, rbf, w1, b1, w2, b2, dist, offs, out):
             nc.vector.tensor_scalar(
                 relu[f][:], lin1_ps[f][:], b1_sb[:, f : f + 1], 0.0, ALU.add, ALU.max
             )
+
+        cosine = held.tile([P, EDGES], F32, name="cosine")
+        nc.scalar.activation(
+            cosine[:], dist_sb[:], ACT.Sin, bias=math.pi / 2, scale=-math.pi / CUTOFF
+        )
         nf_cut = [held.tile([P, EDGES], F32, name=f"nf_cut{m}") for m in range(BLOCKS)]
         for m in range(BLOCKS):
             nc.vector.scalar_tensor_tensor(

@@ -135,7 +135,6 @@ def tile_edge_update_kernel(tc, table, w, rbf, w1, b1, w2, b2, dist, offs, out):
                         stop=(f == BLOCKS - 1),
                     )
 
-        store_queues = [nc.sync, nc.scalar]
         out_sb = [held.tile([P, EDGES], F32, name=f"out_sb{m}") for m in range(BLOCKS)]
         for c, cols in enumerate(HALVES):
             for m in range(BLOCKS):
@@ -147,4 +146,4 @@ def tile_edge_update_kernel(tc, table, w, rbf, w1, b1, w2, b2, dist, offs, out):
                     ALU.add,
                     ALU.mult,
                 )
-                store_queues[m].dma_start(out[m * P : (m + 1) * P, cols], out_sb[m][:, cols])
+                nc.sync.dma_start(out[m * P : (m + 1) * P, cols], out_sb[m][:, cols])

import math

import concourse.mybir as mybir

P = 128
NODES = 1024
EDGES = 512
FEATS = 256
BLOCKS = FEATS // P
CUTOFF = 10.0
HALF = EDGES // 2
HALVES = [slice(0, HALF), slice(HALF, EDGES)]

FILL_MATMULS = 3

ALL_BUT_SIGN = 0x7FFFFFFF

FLOPS = 2 * EDGES * (P * FEATS + FEATS * FEATS + P * FEATS)

BF16, F32, I32, U16 = mybir.dt.bfloat16, mybir.dt.float32, mybir.dt.int32, mybir.dt.uint16
ACT = mybir.ActivationFunctionType
ALU = mybir.AluOpType


def tile_edge_update_kernel(tc, table, w, rbf, w1, b1, w2, b2, dist, offs, out):
    nc = tc.nc
    with (
        tc.tile_pool(name="held", bufs=1) as held,
        tc.psum_pool(name="psum", bufs=1) as psum,
    ):
        silu_col = held.tile([P, 1], F32, name="silu_col")
        nc.vector.memset(silu_col[:], 0.0)
        nc.scalar.activation(silu_col[:], silu_col[:], ACT.Silu)

        zeros = held.tile([P, EDGES], BF16, name="zeros")
        nc.gpsimd.memset(zeros[:], 0.0)

        rbf_sb = held.tile([P, EDGES], BF16, name="rbf_sb")
        nc.sync.dma_start(rbf_sb[:], rbf)
        w1_sb = held.tile([P, FEATS], BF16, name="w1_sb")
        nc.sync.dma_start(w1_sb[:], w1)
        b1_sb = held.tile([P, BLOCKS], F32, name="b1_sb")
        with nc.allow_non_contiguous_dma(reason="one bias element to a partition"):
            nc.sync.dma_start(b1_sb[:], b1.rearrange("(b p) o -> p (b o)", p=P))
        dist_sb = held.tile([P, EDGES], F32, name="dist_sb")
        nc.sync.dma_start(dist_sb[:], dist.broadcast_to([P, EDGES]))
        w_sb = held.tile([P, FEATS], BF16, name="w_sb")
        nc.sync.dma_start(w_sb[:], w)
        offsets = held.tile([P, EDGES // 16], U16, name="offsets")
        nc.sync.dma_start(offsets[:], offs)
        table_sb = held.tile([P, NODES], BF16, name="table_sb")
        nc.sync.dma_start(table_sb[:], table)
        w2_sb = held.tile([P, BLOCKS, FEATS], BF16, name="w2_sb")
        nc.sync.dma_start(w2_sb[:], w2.rearrange("(b p) m -> p b m", p=P))
        b2_sb = held.tile([P, BLOCKS], F32, name="b2_sb")
        with nc.allow_non_contiguous_dma(reason="one bias element to a partition"):
            nc.sync.dma_start(b2_sb[:], b2.rearrange("(b p) o -> p (b o)", p=P))

        lin1_ps = [psum.tile([P, EDGES], F32, name=f"lin1_ps{f}") for f in range(BLOCKS)]
        for fill in range(FILL_MATMULS):
            nc.tensor.matmul(lin1_ps[0][:], zeros[:, :P], zeros[:], start=True, stop=True)
        for f in range(BLOCKS):
            nc.tensor.matmul(
                lin1_ps[f][:], w1_sb[:, f * P : (f + 1) * P], rbf_sb[:], start=True, stop=True
            )

        half_w = held.tile([P, FEATS], BF16, name="half_w")
        nc.vector.tensor_scalar_mul(half_w[:], w_sb[:], 0.5)
        half_nf_ps = [psum.tile([P, EDGES], F32, name=f"half_nf_ps{m}") for m in range(BLOCKS)]
        for m in range(BLOCKS):
            nc.tensor.matmul(
                half_nf_ps[m][:],
                half_w[:, m * P : (m + 1) * P],
                table_sb[:].indirect(offsets[:]),
                start=True,
                stop=True,
            )

        half_b1 = held.tile([P, BLOCKS], F32, name="half_b1")
        nc.vector.tensor_scalar_mul(half_b1[:], b1_sb[:], 0.5)
        tanh = [held.tile([P, EDGES], F32, name=f"tanh{f}") for f in range(BLOCKS)]
        relu = [held.tile([P, EDGES], F32, name=f"relu{f}") for f in range(BLOCKS)]
        abs_tanh = [held.tile([P, EDGES], F32, name=f"abs_tanh{f}") for f in range(BLOCKS)]
        for f in range(BLOCKS):
            nc.scalar.activation(
                tanh[f][:], lin1_ps[f][:], ACT.Tanh, bias=half_b1[:, f : f + 1], scale=0.5
            )
            nc.vector.tensor_scalar(
                abs_tanh[f][:].bitcast(I32),
                tanh[f][:].bitcast(I32),
                ALL_BUT_SIGN,
                None,
                ALU.bitwise_and,
            )
            nc.vector.tensor_scalar(
                relu[f][:], lin1_ps[f][:], b1_sb[:, f : f + 1], 0.0, ALU.add, ALU.max
            )

        cosine = held.tile([P, EDGES], F32, name="cosine")
        nc.scalar.activation(
            cosine[:], dist_sb[:], ACT.Sin, bias=math.pi / 2, scale=-math.pi / CUTOFF
        )
        nf_cut = [held.tile([P, EDGES], F32, name=f"nf_cut{m}") for m in range(BLOCKS)]
        for m in range(BLOCKS):
            nc.vector.scalar_tensor_tensor(
                nf_cut[m][:], cosine[:], 1.0, half_nf_ps[m][:], ALU.add, ALU.mult
            )

        for fill in range(FILL_MATMULS):
            nc.tensor.matmul(lin1_ps[1][:], zeros[:, :P], zeros[:], start=True, stop=True)

        log = [held.tile([P, EDGES], F32, name=f"log{f}") for f in range(BLOCKS)]
        h = [held.tile([P, EDGES], BF16, name=f"h{f}") for f in range(BLOCKS)]
        for cols in HALVES:
            for f in range(BLOCKS):
                nc.scalar.activation(
                    log[f][:, cols], abs_tanh[f][:, cols], ACT.Ln, bias=1.0, scale=1.0
                )
                nc.vector.tensor_tensor(
                    h[f][:, cols], relu[f][:, cols], log[f][:, cols], ALU.subtract
                )

        lin2_ps = [
            [psum.tile([P, HALF], F32, name=f"lin2_ps{m}{c}") for c in range(len(HALVES))]
            for m in range(BLOCKS)
        ]
        for c, cols in enumerate(HALVES):
            for f in range(BLOCKS):
                for m in range(BLOCKS):
                    nc.tensor.matmul(
                        lin2_ps[m][c][:],
                        w2_sb[:, f, m * P : (m + 1) * P],
                        h[f][:, cols],
                        start=(f == 0),
                        stop=(f == BLOCKS - 1),
                    )

        out_sb = [held.tile([P, EDGES], F32, name=f"out_sb{m}") for m in range(BLOCKS)]
        for c, cols in enumerate(HALVES):
            for m in range(BLOCKS):
                nc.vector.scalar_tensor_tensor(
                    out_sb[m][:, cols],
                    lin2_ps[m][c][:],
                    b2_sb[:, m : m + 1],
                    nf_cut[m][:, cols],
                    ALU.add,
                    ALU.mult,
                )
                nc.sync.dma_start(out[m * P : (m + 1) * P, cols], out_sb[m][:, cols])
